import numpy as np
import ml_dtypes


def mxq(x, axis, fmt="e4m3"):
    dtype, down = {"e4m3": (ml_dtypes.float8_e4m3fn, 7), "e5m2": (ml_dtypes.float8_e5m2, 14)}[fmt]
    v = np.moveaxis(np.asarray(x, np.float32).astype(ml_dtypes.bfloat16).astype(np.float64), axis, -1)
    blocks = v.reshape(v.shape[:-1] + (-1, 32))
    amax = np.abs(blocks).max(-1, keepdims=True)
    byte = np.maximum(np.where(amax > 0, np.frexp(amax)[1] - 1 + 127, 0) - down, 1)
    scale = np.exp2(byte - 127.0)
    codes = (blocks / scale).astype(np.float32).astype(dtype).astype(np.float64)
    return np.moveaxis((codes * scale).reshape(v.shape), -1, axis)


WIDE = False


def mx_kscale(k):
    if not WIDE:
        return np.ones(k)
    levels = np.array([10, -10, 5, -5, 0])
    a = np.random.permutation(np.resize(levels, k // 512 * 4)).reshape(k // 512, 4)
    idx = np.arange(k)
    return np.exp2(a[idx // 512, idx % 128 // 32])


BF16 = ml_dtypes.bfloat16


def bf(x):
    return np.asarray(x, np.float32).astype(BF16)


def f64(x):
    return np.asarray(x).astype(np.float64)


B, I, H = 4096, 256, 512


def setup_inputs():
    s = mx_kscale(H)
    w1 = np.concatenate([np.random.standard_normal((H, H)) * 1.5 / np.sqrt(H) / s, np.random.standard_normal(H)[:, None] * 0.6], axis=1)
    return {"h_tilde": bf(np.random.standard_normal((B, H)) * 0.3 * s),
            "k1": bf(np.random.standard_normal((B, H)) * 0.8 * s),
            "k2": bf(np.random.standard_normal((B, H)) * 1.0 * s),
            "k3": bf(np.random.standard_normal((B, H)) * 1.0 * s),
            "t0": bf(0.2 + 0.1 * np.random.random(1)),
            "t1": bf(1.0 + 0.2 * np.random.random(1)),
            "W1": bf(w1),
            "b1": bf(np.random.standard_normal(H) * 0.3),
            "W2": bf(np.random.standard_normal((H, H)) * 1.5 / np.sqrt(H) * s[:, None]),
            "b2": bf(np.random.standard_normal(H) * 0.3 * s)}


def reference(h_tilde, k1, k2, k3, t0, t1, W1, b1, W2, b2):
    dt = f64(t1) - f64(t0)
    t = f64(t0) + dt
    ht = f64(h_tilde)
    y = ht + dt * f64(k3)
    w1 = f64(W1)
    z = np.tanh((mxq(y, 1, "e4m3") @ mxq(w1[:, :H], 1, "e4m3").T) + t * w1[:, H] + f64(b1))
    k4 = (mxq(z, 1, "e4m3") @ mxq(f64(W2), 1, "e4m3").T) + f64(b2)
    return ht + (dt / 6.0) * (f64(k1) + 2.0 * f64(k2) + 2.0 * f64(k3) + k4)

@@ -1,0 +1,283 @@
+from contextlib import ExitStack
+
+import concourse.mybir as mybir
+from concourse.masks import make_identity
+
+F32 = mybir.dt.float32
+BF16 = mybir.dt.bfloat16
+U32 = mybir.dt.uint32
+U8 = mybir.dt.uint8
+FP8X4 = mybir.dt.float8_e4m3fn_x4
+ALU = mybir.AluOpType
+ACT = mybir.ActivationFunctionType
+
+P = 128
+B = 4096
+H = 512
+PACK = 4
+TILES = H // P
+ROWS = 4
+CHUNK = P * ROWS
+CHUNKS = B // CHUNK
+WORDS = H // 2
+STATE_AHEAD = 4
+SLOPE_AHEAD = 3
+
+FLOPS = 2 * 2 * B * H * H
+
+
+def tile_nodelstmcell_pc_t_kernel(tc, h_tilde, k1, k2, k3, t0, t1, W1, b1, W2, b2, out):
+    nc = tc.nc
+    with ExitStack() as stack:
+        const = stack.enter_context(tc.tile_pool(name="const", bufs=1))
+        states = stack.enter_context(tc.tile_pool(name="states", bufs=STATE_AHEAD))
+        slopes = stack.enter_context(tc.tile_pool(name="slopes", bufs=SLOPE_AHEAD))
+        work = stack.enter_context(tc.tile_pool(name="work", bufs=2))
+        psum = stack.enter_context(tc.psum_pool(name="psum", bufs=2))
+
+        live = {}
+
+        def chunk_rows(dram, c):
+            return dram[c * CHUNK : (c + 1) * CHUNK, :].rearrange("(p j) n -> p j n", j=ROWS)
+
+        def flat(tile3):
+            return tile3[:].rearrange("p j n -> p (j n)")
+
+        def load_state(c):
+            k3_sb = states.tile([P, ROWS, H], BF16)
+            nc.sync.dma_start(out=k3_sb[:], in_=chunk_rows(k3, c))
+            ht_sb = states.tile([P, ROWS, H], BF16)
+            nc.sync.dma_start(out=ht_sb[:], in_=chunk_rows(h_tilde, c))
+            live["k3", c] = k3_sb
+            live["ht", c] = ht_sb
+
+        def load_slopes(c):
+            k1_sb = slopes.tile([P, ROWS, H], BF16)
+            nc.sync.dma_start(out=k1_sb[:], in_=chunk_rows(k1, c))
+            k2_sb = slopes.tile([P, ROWS, H], BF16)
+            nc.sync.dma_start(out=k2_sb[:], in_=chunk_rows(k2, c))
+            live["k1", c] = k1_sb
+            live["k2", c] = k2_sb
+
+        t0_sb = const.tile([P, 1], BF16)
+        nc.sync.dma_start(out=t0_sb[:], in_=t0.partition_broadcast(P))
+        t1_sb = const.tile([P, 1], BF16)
+        nc.sync.dma_start(out=t1_sb[:], in_=t1.partition_broadcast(P))
+        load_state(0)
+        w1_sb = const.tile([P, TILES * (H + 2)], BF16)
+        w1_rows = w1_sb[:].rearrange("p (i k) -> p i k", k=H + 2)
+        nc.sync.dma_start(out=w1_rows[:, :, 0 : H + 1], in_=W1.rearrange("(i p) k -> p i k", p=P))
+        load_state(1)
+        bias_rows = const.tile([P, P], BF16)
+        nc.vector.memset(bias_rows[:], 0.0)
+        nc.sync.dma_start(out=bias_rows[0:TILES, :], in_=b1.rearrange("(i p) -> i p", p=P))
+        nc.sync.dma_start(out=bias_rows[TILES : 2 * TILES, :], in_=b2.rearrange("(i p) -> i p", p=P))
+        w2_sb = const.tile([P, TILES, H], BF16)
+        nc.sync.dma_start(out=w2_sb[:], in_=W2.rearrange("(i p) n -> p i n", p=P))
+        load_slopes(0)
+        load_state(2)
+        load_slopes(1)
+        load_state(3)
+        load_slopes(2)
+
+        ident_f32 = const.tile([P, P], F32)
+        make_identity(nc, ident_f32[:])
+        ident_bf16 = const.tile([P, P], BF16)
+        make_identity(nc, ident_bf16[:])
+
+        dt = const.tile([P, 1], F32)
+        nc.vector.tensor_tensor(out=dt[:], in0=t1_sb[:], in1=t0_sb[:], op=ALU.subtract)
+        t_end = const.tile([P, 1], F32)
+        nc.vector.tensor_tensor(out=t_end[:], in0=t0_sb[:], in1=dt[:], op=ALU.add)
+        dt6 = const.tile([P, 1], F32)
+        nc.vector.tensor_scalar_mul(out=dt6[:], in0=dt[:], scalar1=1.0 / 6.0)
+        dt3 = const.tile([P, 1], F32)
+        nc.vector.tensor_scalar_mul(out=dt3[:], in0=dt6[:], scalar1=2.0)
+
+        w1_codes = const.tile([P, H], U32, align_bytes=64)
+        w1_scales = const.tile([P, H], U8, align_bytes=64)
+        w2_codes = const.tile([P, H], U32, align_bytes=64)
+        w2_scales = const.tile([P, H], U8, align_bytes=64)
+        z_bias = const.tile([P, TILES], F32)
+        k4_bias = const.tile([P, TILES], F32)
+
+        def quantise_w1():
+            w1_words = w1_sb[:].bitcast(F32)
+            w1_grouped = const.tile([P, H * PACK], BF16, align_bytes=64)
+            w1_grouped_words = w1_grouped[:].bitcast(F32).rearrange("q (n u) -> q n u", u=2)
+            for half in range(2):
+                w1T_ps = psum.tile([P, 2, 2 * P], F32, tag="turned")
+                for i in range(2):
+                    first = (2 * half + i) * (WORDS + 1)
+                    for u in range(2):
+                        nc.tensor.transpose(
+                            w1T_ps[:, u, i * P : (i + 1) * P],
+                            w1_words[:, first + u * P : first + (u + 1) * P],
+                            ident_f32[:],
+                        )
+                nc.scalar.copy(
+                    out=w1_grouped_words[:, half * 2 * P : (half + 1) * 2 * P, :],
+                    in_=w1T_ps[:].rearrange("q u n -> q n u"),
+                )
+            nc.vector.quantize_mx(out=w1_codes[:].bitcast(FP8X4), scales=w1_scales[:], in_=w1_grouped[:])
+
+        def quantise_w2():
+            w2_grouped = const.tile([P, H * PACK], BF16, align_bytes=64)
+            w2_grouped_cols = w2_grouped[:].rearrange("p (o i) -> p o i", i=PACK)
+            for half in range(2):
+                w2T_ps = psum.tile([P, PACK, 2 * P], BF16, tag="turned")
+                for m in range(2):
+                    for i in range(PACK):
+                        nc.tensor.transpose(
+                            w2T_ps[:, i, m * P : (m + 1) * P],
+                            w2_sb[:, 2 * half + m, i * P : (i + 1) * P],
+                            ident_bf16[:],
+                        )
+                nc.scalar.copy(
+                    out=w2_grouped_cols[:, half * 2 * P : (half + 1) * 2 * P, :],
+                    in_=w2T_ps[:].rearrange("p i o -> p o i"),
+                )
+            nc.vector.quantize_mx(out=w2_codes[:].bitcast(FP8X4), scales=w2_scales[:], in_=w2_grouped[:])
+
+        def biases_to_partitions():
+            biasT_ps = psum.tile([P, P], BF16, tag="turned")
+            nc.tensor.transpose(biasT_ps[:], bias_rows[:], ident_bf16[:])
+            bias_cols = const.tile([P, 2 * TILES], F32)
+            nc.vector.tensor_copy(out=bias_cols[:], in_=biasT_ps[:, 0 : 2 * TILES])
+            nc.vector.scalar_tensor_tensor(
+                out=z_bias[:], in0=w1_rows[:, :, H], scalar=t_end[:, 0:1], in1=bias_cols[:, 0:TILES],
+                op0=ALU.mult, op1=ALU.add,
+            )
+            nc.vector.tensor_scalar_mul(out=k4_bias[:], in0=bias_cols[:, TILES : 2 * TILES], scalar1=dt6[:, 0:1])
+
+        def state_to_columns(c):
+            y_sb = work.tile([P, ROWS * H], BF16)
+            nc.vector.scalar_tensor_tensor(
+                out=y_sb[:], in0=flat(live["k3", c]), scalar=dt[:, 0:1], in1=flat(live["ht", c]),
+                op0=ALU.mult, op1=ALU.add,
+            )
+            y_words = y_sb[:].bitcast(F32)
+            y_grouped = work.tile([P, CHUNK * PACK], BF16, align_bytes=64)
+            y_grouped_words = y_grouped[:].bitcast(F32).rearrange("q (b u) -> q b u", u=2)
+            for half in range(2):
+                yT_ps = psum.tile([P, 2, 2 * P], F32, tag="turned")
+                for i in range(2):
+                    first = (2 * half + i) * WORDS
+                    for u in range(2):
+                        nc.tensor.transpose(
+                            yT_ps[:, u, i * P : (i + 1) * P],
+                            y_words[:, first + u * P : first + (u + 1) * P],
+                            ident_f32[:],
+                        )
+                nc.scalar.copy(
+                    out=y_grouped_words[:, half * 2 * P : (half + 1) * 2 * P, :],
+                    in_=yT_ps[:].rearrange("q u b -> q b u"),
+                )
+            live["y_grouped", c] = y_grouped
+
+        def first_layer(c):
+            y_codes = work.tile([P, CHUNK], U32, align_bytes=64)
+            y_scales = work.tile([P, CHUNK], U8, align_bytes=64)
+            nc.vector.quantize_mx(out=y_codes[:].bitcast(FP8X4), scales=y_scales[:], in_=live["y_grouped", c][:])
+            zT_sb = work.tile([P, PACK, CHUNK], BF16)
+            for i in range(TILES):
+                pre_ps = psum.tile([P, CHUNK], F32, tag="pre")
+                nc.tensor.matmul_mx(
+                    out=pre_ps[:],
+                    lhsT=w1_codes[:, i * P : (i + 1) * P].bitcast(FP8X4),
+                    lhsT_scale=w1_scales[:, i * P : (i + 1) * P],
+                    rhs=y_codes[:].bitcast(FP8X4),
+                    rhs_scale=y_scales[:],
+                    start=True,
+                    stop=True,
+                )
+                nc.scalar.activation(out=zT_sb[:, i, :], in_=pre_ps[:], func=ACT.Tanh, bias=z_bias[:, i : i + 1], scale=1.0)
+            z_grouped = work.tile([P, CHUNK * PACK], BF16, align_bytes=64)
+            nc.scalar.copy(
+                out=z_grouped[:].rearrange("p (c r i) -> p c i r", r=4, i=PACK),
+                in_=zT_sb[:].rearrange("p i (c r) -> p c i r", r=4),
+            )
+            live["z_grouped", c] = z_grouped
+
+        def second_layer(c):
+            z_codes = work.tile([P, CHUNK], U32, align_bytes=64)
+            z_scales = work.tile([P, CHUNK], U8, align_bytes=64)
+            nc.vector.quantize_mx(out=z_codes[:].bitcast(FP8X4), scales=z_scales[:], in_=live["z_grouped", c][:])
+            k4T_sb = work.tile([P, TILES, CHUNK], F32)
+            for m in range(TILES):
+                k4T_ps = psum.tile([P, CHUNK], F32, tag="k4T")
+                nc.tensor.matmul_mx(
+                    out=k4T_ps[:],
+                    lhsT=w2_codes[:, m * P : (m + 1) * P].bitcast(FP8X4),
+                    lhsT_scale=w2_scales[:, m * P : (m + 1) * P],
+                    rhs=z_codes[:].bitcast(FP8X4),
+                    rhs_scale=z_scales[:],
+                    start=True,
+                    stop=True,
+                )
+                nc.scalar.activation(
+                    out=k4T_sb[:, m, :], in_=k4T_ps[:], func=ACT.Identity, bias=k4_bias[:, m : m + 1], scale=dt6[:, 0:1]
+                )
+            live["k4T", c] = k4T_sb
+
+        def turn_k1(c):
+            k1_sb = live["k1", c]
+            k1T_sb = work.tile([P, TILES, CHUNK], F32)
+            for half in range(2):
+                k1T_ps = psum.tile([P, 2, CHUNK], BF16, tag="turned")
+                for i in range(2):
+                    m = 2 * half + i
+                    for j in range(ROWS):
+                        nc.tensor.transpose(
+                            k1T_ps[:, i, j * P : (j + 1) * P], k1_sb[:, j, m * P : (m + 1) * P], ident_bf16[:]
+                        )
+                nc.scalar.activation(
+                    out=k1T_sb[:, 2 * half : 2 * half + 2, :], in_=k1T_ps[:], func=ACT.Copy, scale=dt6[:, 0:1]
+                )
+            live["k1T", c] = k1T_sb
+
+        def sum_on_vector(c):
+            total = work.tile([P, ROWS, H], F32, bufs=3)
+            nc.vector.tensor_tensor(out=flat(total), in0=flat(live["k2", c]), in1=flat(live["k3", c]), op=ALU.add)
+            nc.vector.scalar_tensor_tensor(
+                out=flat(total), in0=flat(total), scalar=dt3[:, 0:1], in1=flat(live["ht", c]), op0=ALU.mult, op1=ALU.add
+            )
+            live["total", c] = total
+
+        def finish(c):
+            total = live["total", c]
+            for j in range(ROWS):
+                back_ps = psum.tile([P, H], F32, tag="back")
+                for m in range(TILES):
+                    nc.tensor.matmul(
+                        out=back_ps[:, m * P : (m + 1) * P], lhsT=live["k4T", c][:, m, j * P : (j + 1) * P],
+                        rhs=ident_f32[:], start=True, stop=False, is_transpose=True,
+                    )
+                    nc.tensor.matmul(
+                        out=back_ps[:, m * P : (m + 1) * P], lhsT=live["k1T", c][:, m, j * P : (j + 1) * P],
+                        rhs=ident_f32[:], start=False, stop=True, is_transpose=True,
+                    )
+                nc.vector.tensor_tensor(out=total[:, j, :], in0=back_ps[:], in1=total[:, j, :], op=ALU.add)
+            nc.sync.dma_start(out=chunk_rows(out, c), in_=total[:])
+
+        state_to_columns(0)
+        quantise_w1()
+        state_to_columns(1)
+        biases_to_partitions()
+        first_layer(0)
+        quantise_w2()
+        turn_k1(0)
+        for step in range(CHUNKS):
+            second_layer(step)
+            if step + 1 < CHUNKS:
+                first_layer(step + 1)
+            if step + 2 < CHUNKS:
+                state_to_columns(step + 2)
+            sum_on_vector(step)
+            finish(step)
+            if step + 1 < CHUNKS:
+                turn_k1(step + 1)
+            if step + STATE_AHEAD < CHUNKS:
+                load_state(step + STATE_AHEAD)
+            if step + SLOPE_AHEAD < CHUNKS:
+                load_slopes(step + SLOPE_AHEAD)

@@ -22,6 +22,7 @@ CHUNKS = B // CHUNK
 WORDS = H // 2
 STATE_AHEAD = 4
 SLOPE_AHEAD = 3
+PLAIN_ROWS = 3
 
 FLOPS = 2 * 2 * B * H * H
 
@@ -148,7 +149,7 @@ def tile_nodelstmcell_pc_t_kernel(tc, h_tilde, k1, k2, k3, t0, t1, W1, b1, W2, b
                 out=z_bias[:], in0=w1_rows[:, :, H], scalar=t_end[:, 0:1], in1=bias_cols[:, 0:TILES],
                 op0=ALU.mult, op1=ALU.add,
             )
-            nc.vector.tensor_scalar_mul(out=k4_bias[:], in0=bias_cols[:, TILES : 2 * TILES], scalar1=dt6[:, 0:1])
+            nc.vector.tensor_copy(out=k4_bias[:], in_=bias_cols[:, TILES : 2 * TILES])
 
         def state_to_columns(c):
             y_sb = work.tile([P, ROWS * H], BF16)
@@ -216,24 +217,18 @@ def tile_nodelstmcell_pc_t_kernel(tc, h_tilde, k1, k2, k3, t0, t1, W1, b1, W2, b
                     stop=True,
                 )
                 nc.scalar.activation(
-                    out=k4T_sb[:, m, :], in_=k4T_ps[:], func=ACT.Identity, bias=k4_bias[:, m : m + 1], scale=dt6[:, 0:1]
+                    out=k4T_sb[:, m, :], in_=k4T_ps[:], func=ACT.Identity, bias=k4_bias[:, m : m + 1], scale=1.0
                 )
             live["k4T", c] = k4T_sb
 
         def turn_k1(c):
             k1_sb = live["k1", c]
-            k1T_sb = work.tile([P, TILES, CHUNK], F32)
-            for half in range(2):
-                k1T_ps = psum.tile([P, 2, CHUNK], BF16, tag="turned")
-                for i in range(2):
-                    m = 2 * half + i
-                    for j in range(ROWS):
-                        nc.tensor.transpose(
-                            k1T_ps[:, i, j * P : (j + 1) * P], k1_sb[:, j, m * P : (m + 1) * P], ident_bf16[:]
-                        )
-                nc.scalar.activation(
-                    out=k1T_sb[:, 2 * half : 2 * half + 2, :], in_=k1T_ps[:], func=ACT.Copy, scale=dt6[:, 0:1]
-                )
+            k1T_sb = work.tile([P, ROWS - PLAIN_ROWS, TILES, P], F32)
+            for j in range(PLAIN_ROWS, ROWS):
+                k1T_ps = psum.tile([P, TILES, P], BF16, tag="turned")
+                for m in range(TILES):
+                    nc.tensor.transpose(k1T_ps[:, m, :], k1_sb[:, j, m * P : (m + 1) * P], ident_bf16[:])
+                nc.scalar.copy(out=k1T_sb[:, j - PLAIN_ROWS, :, :], in_=k1T_ps[:])
             live["k1T", c] = k1T_sb
 
         def sum_on_vector(c):
@@ -248,16 +243,22 @@ def tile_nodelstmcell_pc_t_kernel(tc, h_tilde, k1, k2, k3, t0, t1, W1, b1, W2, b
             total = live["total", c]
             for j in range(ROWS):
                 back_ps = psum.tile([P, H], F32, tag="back")
+                if j < PLAIN_ROWS:
+                    nc.tensor.matmul(out=back_ps[:], lhsT=ident_bf16[:], rhs=live["k1", c][:, j, :], start=True, stop=False)
+                else:
+                    for m in range(TILES):
+                        nc.tensor.matmul(
+                            out=back_ps[:, m * P : (m + 1) * P], lhsT=live["k1T", c][:, j - PLAIN_ROWS, m, :],
+                            rhs=ident_f32[:], start=(m == 0), stop=False, is_transpose=True,
+                        )
                 for m in range(TILES):
                     nc.tensor.matmul(
                         out=back_ps[:, m * P : (m + 1) * P], lhsT=live["k4T", c][:, m, j * P : (j + 1) * P],
-                        rhs=ident_f32[:], start=True, stop=False, is_transpose=True,
+                        rhs=ident_f32[:], start=False, stop=(m == TILES - 1), is_transpose=True,
                     )
-                    nc.tensor.matmul(
-                        out=back_ps[:, m * P : (m + 1) * P], lhsT=live["k1T", c][:, m, j * P : (j + 1) * P],
-                        rhs=ident_f32[:], start=False, stop=True, is_transpose=True,
-                    )
-                nc.vector.tensor_tensor(out=total[:, j, :], in0=back_ps[:], in1=total[:, j, :], op=ALU.add)
+                nc.vector.scalar_tensor_tensor(
+                    out=total[:, j, :], in0=back_ps[:], scalar=dt6[:, 0:1], in1=total[:, j, :], op0=ALU.mult, op1=ALU.add
+                )
             nc.sync.dma_start(out=chunk_rows(out, c), in_=total[:])
 
         state_to_columns(0)

@@ -221,21 +221,29 @@ def tile_nodelstmcell_pc_t_kernel(tc, h_tilde, k1, k2, k3, t0, t1, W1, b1, W2, b
                 )
             live["k4T", c] = k4T_sb
 
-        def turn_k1(c):
-            k1_sb = live["k1", c]
-            k1T_sb = work.tile([P, ROWS - PLAIN_ROWS, TILES, P], F32)
-            for j in range(PLAIN_ROWS, ROWS):
-                k1T_ps = psum.tile([P, TILES, P], BF16, tag="turned")
+        def turn_slopes(c):
+            slopesT_sb = work.tile([P, 3, TILES, P], F32)
+            k1T_ps = psum.tile([P, TILES, P], BF16, tag="turned")
+            for m in range(TILES):
+                nc.tensor.transpose(k1T_ps[:, m, :], live["k1", c][:, PLAIN_ROWS, m * P : (m + 1) * P], ident_bf16[:])
+            nc.scalar.copy(out=slopesT_sb[:, 0, :, :], in_=k1T_ps[:])
+            k23T_ps = psum.tile([P, 2, TILES, P], BF16, tag="turned")
+            for a, name in enumerate(("k2", "k3")):
                 for m in range(TILES):
-                    nc.tensor.transpose(k1T_ps[:, m, :], k1_sb[:, j, m * P : (m + 1) * P], ident_bf16[:])
-                nc.scalar.copy(out=k1T_sb[:, j - PLAIN_ROWS, :, :], in_=k1T_ps[:])
-            live["k1T", c] = k1T_sb
+                    nc.tensor.transpose(
+                        k23T_ps[:, a, m, :], live[name, c][:, PLAIN_ROWS, m * P : (m + 1) * P], ident_bf16[:]
+                    )
+            nc.scalar.activation(out=slopesT_sb[:, 1:3, :, :], in_=k23T_ps[:], func=ACT.Copy, scale=2.0)
+            live["slopesT", c] = slopesT_sb
 
         def sum_on_vector(c):
+            def part(tile3):
+                return tile3[:, 0:PLAIN_ROWS, :].rearrange("p j n -> p (j n)")
+
             total = work.tile([P, ROWS, H], F32, bufs=3)
-            nc.vector.tensor_tensor(out=flat(total), in0=flat(live["k2", c]), in1=flat(live["k3", c]), op=ALU.add)
+            nc.vector.tensor_tensor(out=part(total), in0=part(live["k2", c]), in1=part(live["k3", c]), op=ALU.add)
             nc.vector.scalar_tensor_tensor(
-                out=flat(total), in0=flat(total), scalar=dt3[:, 0:1], in1=flat(live["ht", c]), op0=ALU.mult, op1=ALU.add
+                out=part(total), in0=part(total), scalar=dt3[:, 0:1], in1=part(live["ht", c]), op0=ALU.mult, op1=ALU.add
             )
             live["total", c] = total
 
@@ -245,21 +253,24 @@ def tile_nodelstmcell_pc_t_kernel(tc, h_tilde, k1, k2, k3, t0, t1, W1, b1, W2, b
                 back_ps = psum.tile([P, H], F32, tag="back")
                 if j < PLAIN_ROWS:
                     nc.tensor.matmul(out=back_ps[:], lhsT=ident_bf16[:], rhs=live["k1", c][:, j, :], start=True, stop=False)
+                    rest = total[:, j, :]
                 else:
-                    for m in range(TILES):
-                        nc.tensor.matmul(
-                            out=back_ps[:, m * P : (m + 1) * P], lhsT=live["k1T", c][:, j - PLAIN_ROWS, m, :],
-                            rhs=ident_f32[:], start=(m == 0), stop=False, is_transpose=True,
-                        )
+                    for a in range(3):
+                        for m in range(TILES):
+                            nc.tensor.matmul(
+                                out=back_ps[:, m * P : (m + 1) * P], lhsT=live["slopesT", c][:, a, m, :],
+                                rhs=ident_f32[:], start=(a == 0 and m == 0), stop=False, is_transpose=True,
+                            )
+                    rest = live["ht", c][:, j, :]
                 for m in range(TILES):
                     nc.tensor.matmul(
                         out=back_ps[:, m * P : (m + 1) * P], lhsT=live["k4T", c][:, m, j * P : (j + 1) * P],
                         rhs=ident_f32[:], start=False, stop=(m == TILES - 1), is_transpose=True,
                     )
                 nc.vector.scalar_tensor_tensor(
-                    out=total[:, j, :], in0=back_ps[:], scalar=dt6[:, 0:1], in1=total[:, j, :], op0=ALU.mult, op1=ALU.add
+                    out=total[:, j, :], in0=back_ps[:], scalar=dt6[:, 0:1], in1=rest, op0=ALU.mult, op1=ALU.add
                 )
-            nc.sync.dma_start(out=chunk_rows(out, c), in_=total[:])
+                nc.sync.dma_start(out=chunk_rows(out, c)[:, j, :], in_=total[:, j, :])
 
         state_to_columns(0)
         quantise_w1()
@@ -267,7 +278,7 @@ def tile_nodelstmcell_pc_t_kernel(tc, h_tilde, k1, k2, k3, t0, t1, W1, b1, W2, b
         biases_to_partitions()
         first_layer(0)
         quantise_w2()
-        turn_k1(0)
+        turn_slopes(0)
         for step in range(CHUNKS):
             second_layer(step)
             if step + 1 < CHUNKS:
@@ -277,7 +288,7 @@ def tile_nodelstmcell_pc_t_kernel(tc, h_tilde, k1, k2, k3, t0, t1, W1, b1, W2, b
             sum_on_vector(step)
             finish(step)
             if step + 1 < CHUNKS:
-                turn_k1(step + 1)
+                turn_slopes(step + 1)
             if step + STATE_AHEAD < CHUNKS:
                 load_state(step + STATE_AHEAD)
             if step + SLOPE_AHEAD < CHUNKS:

@@ -20,7 +20,7 @@ ROWS = 4
 CHUNK = P * ROWS
 CHUNKS = B // CHUNK
 WORDS = H // 2
-STATE_AHEAD = 4
+STATE_AHEAD = 5
 SLOPE_AHEAD = 3
 PLAIN_ROWS = 3
 
@@ -80,6 +80,7 @@ def tile_nodelstmcell_pc_t_kernel(tc, h_tilde, k1, k2, k3, t0, t1, W1, b1, W2, b
         load_slopes(1)
         load_state(3)
         load_slopes(2)
+        load_state(4)
 
         ident_f32 = const.tile([P, P], F32)
         make_identity(nc, ident_f32[:])
@@ -158,7 +159,7 @@ def tile_nodelstmcell_pc_t_kernel(tc, h_tilde, k1, k2, k3, t0, t1, W1, b1, W2, b
                 op0=ALU.mult, op1=ALU.add,
             )
             y_words = y_sb[:].bitcast(F32)
-            y_grouped = work.tile([P, CHUNK * PACK], BF16, align_bytes=64)
+            y_grouped = work.tile([P, CHUNK * PACK], BF16, align_bytes=64, bufs=3)
             y_grouped_words = y_grouped[:].bitcast(F32).rearrange("q (b u) -> q b u", u=2)
             for half in range(2):
                 yT_ps = psum.tile([P, 2, 2 * P], F32, tag="turned")
@@ -193,7 +194,7 @@ def tile_nodelstmcell_pc_t_kernel(tc, h_tilde, k1, k2, k3, t0, t1, W1, b1, W2, b
                     stop=True,
                 )
                 nc.scalar.activation(out=zT_sb[:, i, :], in_=pre_ps[:], func=ACT.Tanh, bias=z_bias[:, i : i + 1], scale=1.0)
-            z_grouped = work.tile([P, CHUNK * PACK], BF16, align_bytes=64)
+            z_grouped = work.tile([P, CHUNK * PACK], BF16, align_bytes=64, bufs=3)
             nc.scalar.copy(
                 out=z_grouped[:].rearrange("p (c r i) -> p c i r", r=4, i=PACK),
                 in_=zT_sb[:].rearrange("p i (c r) -> p c i r", r=4),
@@ -204,7 +205,7 @@ def tile_nodelstmcell_pc_t_kernel(tc, h_tilde, k1, k2, k3, t0, t1, W1, b1, W2, b
             z_codes = work.tile([P, CHUNK], U32, align_bytes=64)
             z_scales = work.tile([P, CHUNK], U8, align_bytes=64)
             nc.vector.quantize_mx(out=z_codes[:].bitcast(FP8X4), scales=z_scales[:], in_=live["z_grouped", c][:])
-            k4T_sb = work.tile([P, TILES, CHUNK], F32)
+            k4T_sb = work.tile([P, TILES, CHUNK], F32, bufs=3)
             for m in range(TILES):
                 k4T_ps = psum.tile([P, CHUNK], F32, tag="k4T")
                 nc.tensor.matmul_mx(
@@ -221,31 +222,26 @@ def tile_nodelstmcell_pc_t_kernel(tc, h_tilde, k1, k2, k3, t0, t1, W1, b1, W2, b
                 )
             live["k4T", c] = k4T_sb
 
-        def turn_slopes(c):
-            slopesT_sb = work.tile([P, 3, TILES, P], F32)
-            k1T_ps = psum.tile([P, TILES, P], BF16, tag="turned")
-            for m in range(TILES):
-                nc.tensor.transpose(k1T_ps[:, m, :], live["k1", c][:, PLAIN_ROWS, m * P : (m + 1) * P], ident_bf16[:])
-            nc.scalar.copy(out=slopesT_sb[:, 0, :, :], in_=k1T_ps[:])
-            k23T_ps = psum.tile([P, 2, TILES, P], BF16, tag="turned")
-            for a, name in enumerate(("k2", "k3")):
+        def turn_k1(c):
+            k1_sb = live["k1", c]
+            k1T_sb = work.tile([P, ROWS - PLAIN_ROWS, TILES, P], F32, bufs=3)
+            for j in range(PLAIN_ROWS, ROWS):
+                k1T_ps = psum.tile([P, TILES, P], BF16, tag="turned")
                 for m in range(TILES):
-                    nc.tensor.transpose(
-                        k23T_ps[:, a, m, :], live[name, c][:, PLAIN_ROWS, m * P : (m + 1) * P], ident_bf16[:]
-                    )
-            nc.scalar.activation(out=slopesT_sb[:, 1:3, :, :], in_=k23T_ps[:], func=ACT.Copy, scale=2.0)
-            live["slopesT", c] = slopesT_sb
+                    nc.tensor.transpose(k1T_ps[:, m, :], k1_sb[:, j, m * P : (m + 1) * P], ident_bf16[:])
+                nc.scalar.copy(out=k1T_sb[:, j - PLAIN_ROWS, :, :], in_=k1T_ps[:])
+            live["k1T", c] = k1T_sb
 
-        def sum_on_vector(c):
-            def part(tile3):
-                return tile3[:, 0:PLAIN_ROWS, :].rearrange("p j n -> p (j n)")
-
-            total = work.tile([P, ROWS, H], F32, bufs=3)
-            nc.vector.tensor_tensor(out=part(total), in0=part(live["k2", c]), in1=part(live["k3", c]), op=ALU.add)
-            nc.vector.scalar_tensor_tensor(
-                out=part(total), in0=part(total), scalar=dt3[:, 0:1], in1=part(live["ht", c]), op0=ALU.mult, op1=ALU.add
-            )
+        def add_slopes(c):
+            total = work.tile([P, ROWS, H], F32, bufs=4)
+            nc.vector.tensor_tensor(out=flat(total), in0=flat(live["k2", c]), in1=flat(live["k3", c]), op=ALU.add)
             live["total", c] = total
+
+        def add_state(c):
+            total = live["total", c]
+            nc.vector.scalar_tensor_tensor(
+                out=flat(total), in0=flat(total), scalar=dt3[:, 0:1], in1=flat(live["ht", c]), op0=ALU.mult, op1=ALU.add
+            )
 
         def finish(c):
             total = live["total", c]
@@ -253,43 +249,46 @@ def tile_nodelstmcell_pc_t_kernel(tc, h_tilde, k1, k2, k3, t0, t1, W1, b1, W2, b
                 back_ps = psum.tile([P, H], F32, tag="back")
                 if j < PLAIN_ROWS:
                     nc.tensor.matmul(out=back_ps[:], lhsT=ident_bf16[:], rhs=live["k1", c][:, j, :], start=True, stop=False)
-                    rest = total[:, j, :]
                 else:
-                    for a in range(3):
-                        for m in range(TILES):
-                            nc.tensor.matmul(
-                                out=back_ps[:, m * P : (m + 1) * P], lhsT=live["slopesT", c][:, a, m, :],
-                                rhs=ident_f32[:], start=(a == 0 and m == 0), stop=False, is_transpose=True,
-                            )
-                    rest = live["ht", c][:, j, :]
+                    for m in range(TILES):
+                        nc.tensor.matmul(
+                            out=back_ps[:, m * P : (m + 1) * P], lhsT=live["k1T", c][:, j - PLAIN_ROWS, m, :],
+                            rhs=ident_f32[:], start=(m == 0), stop=False, is_transpose=True,
+                        )
                 for m in range(TILES):
                     nc.tensor.matmul(
                         out=back_ps[:, m * P : (m + 1) * P], lhsT=live["k4T", c][:, m, j * P : (j + 1) * P],
                         rhs=ident_f32[:], start=False, stop=(m == TILES - 1), is_transpose=True,
                     )
                 nc.vector.scalar_tensor_tensor(
-                    out=total[:, j, :], in0=back_ps[:], scalar=dt6[:, 0:1], in1=rest, op0=ALU.mult, op1=ALU.add
+                    out=total[:, j, :], in0=back_ps[:], scalar=dt6[:, 0:1], in1=total[:, j, :], op0=ALU.mult, op1=ALU.add
                 )
                 nc.sync.dma_start(out=chunk_rows(out, c)[:, j, :], in_=total[:, j, :])
 
+        def chunks_at(c):
+            return [c] if 0 <= c < CHUNKS else []
+
         state_to_columns(0)
         quantise_w1()
-        state_to_columns(1)
         biases_to_partitions()
         first_layer(0)
+        state_to_columns(1)
         quantise_w2()
-        turn_slopes(0)
-        for step in range(CHUNKS):
-            second_layer(step)
-            if step + 1 < CHUNKS:
-                first_layer(step + 1)
-            if step + 2 < CHUNKS:
-                state_to_columns(step + 2)
-            sum_on_vector(step)
-            finish(step)
-            if step + 1 < CHUNKS:
-                turn_slopes(step + 1)
-            if step + STATE_AHEAD < CHUNKS:
-                load_state(step + STATE_AHEAD)
-            if step + SLOPE_AHEAD < CHUNKS:
-                load_slopes(step + SLOPE_AHEAD)
+        for step in range(-1, CHUNKS):
+            for c in chunks_at(step + 1):
+                second_layer(c)
+            for c in chunks_at(step + 2):
+                first_layer(c)
+            for c in chunks_at(step + 1):
+                add_slopes(c)
+            for c in chunks_at(step + 3):
+                state_to_columns(c)
+            for c in chunks_at(step + 1):
+                turn_k1(c)
+            for c in chunks_at(step):
+                add_state(c)
+                finish(c)
+                for later in chunks_at(c + STATE_AHEAD):
+                    load_state(later)
+                for later in chunks_at(c + SLOPE_AHEAD):
+                    load_slopes(later)

@@ -22,7 +22,8 @@ CHUNKS = B // CHUNK
 WORDS = H // 2
 STATE_AHEAD = 5
 SLOPE_AHEAD = 3
-PLAIN_ROWS = 3
+LAST = ROWS - 1
+SCALAR_RUNS = 64
 
 FLOPS = 2 * 2 * B * H * H
 
@@ -41,14 +42,20 @@ def tile_nodelstmcell_pc_t_kernel(tc, h_tilde, k1, k2, k3, t0, t1, W1, b1, W2, b
         def chunk_rows(dram, c):
             return dram[c * CHUNK : (c + 1) * CHUNK, :].rearrange("(p j) n -> p j n", j=ROWS)
 
-        def flat(tile3):
-            return tile3[:].rearrange("p j n -> p (j n)")
+        def flat(rows):
+            return rows.rearrange("p j n -> p (j n)")
+
+        def most(tile3):
+            return flat(tile3[:, 0:LAST, :])
 
         def load_state(c):
             k3_sb = states.tile([P, ROWS, H], BF16)
-            nc.sync.dma_start(out=k3_sb[:], in_=chunk_rows(k3, c))
             ht_sb = states.tile([P, ROWS, H], BF16)
-            nc.sync.dma_start(out=ht_sb[:], in_=chunk_rows(h_tilde, c))
+            parts = 2 if c == 0 else 1
+            for part in range(parts):
+                rows = slice(part * ROWS // parts, (part + 1) * ROWS // parts)
+                nc.sync.dma_start(out=k3_sb[:, rows, :], in_=chunk_rows(k3, c)[:, rows, :])
+                nc.sync.dma_start(out=ht_sb[:, rows, :], in_=chunk_rows(h_tilde, c)[:, rows, :])
             live["k3", c] = k3_sb
             live["ht", c] = ht_sb
 
@@ -61,9 +68,9 @@ def tile_nodelstmcell_pc_t_kernel(tc, h_tilde, k1, k2, k3, t0, t1, W1, b1, W2, b
             live["k2", c] = k2_sb
 
         t0_sb = const.tile([P, 1], BF16)
-        nc.sync.dma_start(out=t0_sb[:], in_=t0.partition_broadcast(P))
+        nc.scalar.dma_start(out=t0_sb[:], in_=t0.partition_broadcast(P))
         t1_sb = const.tile([P, 1], BF16)
-        nc.sync.dma_start(out=t1_sb[:], in_=t1.partition_broadcast(P))
+        nc.scalar.dma_start(out=t1_sb[:], in_=t1.partition_broadcast(P))
         load_state(0)
         w1_sb = const.tile([P, TILES * (H + 2)], BF16)
         w1_rows = w1_sb[:].rearrange("p (i k) -> p i k", k=H + 2)
@@ -86,15 +93,15 @@ def tile_nodelstmcell_pc_t_kernel(tc, h_tilde, k1, k2, k3, t0, t1, W1, b1, W2, b
         make_identity(nc, ident_f32[:])
         ident_bf16 = const.tile([P, P], BF16)
         make_identity(nc, ident_bf16[:])
+        half_ident = const.tile([P, P], BF16)
+        nc.vector.tensor_scalar_mul(out=half_ident[:], in0=ident_bf16[:], scalar1=0.5)
 
         dt = const.tile([P, 1], F32)
         nc.vector.tensor_tensor(out=dt[:], in0=t1_sb[:], in1=t0_sb[:], op=ALU.subtract)
         t_end = const.tile([P, 1], F32)
         nc.vector.tensor_tensor(out=t_end[:], in0=t0_sb[:], in1=dt[:], op=ALU.add)
-        dt6 = const.tile([P, 1], F32)
-        nc.vector.tensor_scalar_mul(out=dt6[:], in0=dt[:], scalar1=1.0 / 6.0)
         dt3 = const.tile([P, 1], F32)
-        nc.vector.tensor_scalar_mul(out=dt3[:], in0=dt6[:], scalar1=2.0)
+        nc.vector.tensor_scalar_mul(out=dt3[:], in0=dt[:], scalar1=1.0 / 3.0)
 
         w1_codes = const.tile([P, H], U32, align_bytes=64)
         w1_scales = const.tile([P, H], U8, align_bytes=64)
@@ -135,9 +142,11 @@ def tile_nodelstmcell_pc_t_kernel(tc, h_tilde, k1, k2, k3, t0, t1, W1, b1, W2, b
                             w2_sb[:, 2 * half + m, i * P : (i + 1) * P],
                             ident_bf16[:],
                         )
-                nc.scalar.copy(
+                nc.scalar.activation(
                     out=w2_grouped_cols[:, half * 2 * P : (half + 1) * 2 * P, :],
                     in_=w2T_ps[:].rearrange("p i o -> p o i"),
+                    func=ACT.Copy,
+                    scale=0.5,
                 )
             nc.vector.quantize_mx(out=w2_codes[:].bitcast(FP8X4), scales=w2_scales[:], in_=w2_grouped[:])
 
@@ -150,14 +159,16 @@ def tile_nodelstmcell_pc_t_kernel(tc, h_tilde, k1, k2, k3, t0, t1, W1, b1, W2, b
                 out=z_bias[:], in0=w1_rows[:, :, H], scalar=t_end[:, 0:1], in1=bias_cols[:, 0:TILES],
                 op0=ALU.mult, op1=ALU.add,
             )
-            nc.vector.tensor_copy(out=k4_bias[:], in_=bias_cols[:, TILES : 2 * TILES])
+            nc.vector.tensor_scalar_mul(out=k4_bias[:], in0=bias_cols[:, TILES : 2 * TILES], scalar1=0.5)
 
         def state_to_columns(c):
             y_sb = work.tile([P, ROWS * H], BF16)
-            nc.vector.scalar_tensor_tensor(
-                out=y_sb[:], in0=flat(live["k3", c]), scalar=dt[:, 0:1], in1=flat(live["ht", c]),
-                op0=ALU.mult, op1=ALU.add,
-            )
+            for half in range(2):
+                rows = slice(2 * half, 2 * half + 2)
+                nc.vector.scalar_tensor_tensor(
+                    out=y_sb[:, 2 * half * H : 2 * (half + 1) * H], in0=flat(live["k3", c][:, rows, :]), scalar=dt[:, 0:1],
+                    in1=flat(live["ht", c][:, rows, :]), op0=ALU.mult, op1=ALU.add,
+                )
             y_words = y_sb[:].bitcast(F32)
             y_grouped = work.tile([P, CHUNK * PACK], BF16, align_bytes=64, bufs=3)
             y_grouped_words = y_grouped[:].bitcast(F32).rearrange("q (b u) -> q b u", u=2)
@@ -195,10 +206,10 @@ def tile_nodelstmcell_pc_t_kernel(tc, h_tilde, k1, k2, k3, t0, t1, W1, b1, W2, b
                 )
                 nc.scalar.activation(out=zT_sb[:, i, :], in_=pre_ps[:], func=ACT.Tanh, bias=z_bias[:, i : i + 1], scale=1.0)
             z_grouped = work.tile([P, CHUNK * PACK], BF16, align_bytes=64, bufs=3)
-            nc.scalar.copy(
-                out=z_grouped[:].rearrange("p (c r i) -> p c i r", r=4, i=PACK),
-                in_=zT_sb[:].rearrange("p i (c r) -> p c i r", r=4),
-            )
+            grouped_view = z_grouped[:].rearrange("p (c r i) -> p c i r", r=4, i=PACK)
+            tile_view = zT_sb[:].rearrange("p i (c r) -> p c i r", r=4)
+            nc.scalar.copy(out=grouped_view[:, 0:SCALAR_RUNS, :, :], in_=tile_view[:, 0:SCALAR_RUNS, :, :])
+            nc.vector.tensor_copy(out=grouped_view[:, SCALAR_RUNS:, :, :], in_=tile_view[:, SCALAR_RUNS:, :, :])
             live["z_grouped", c] = z_grouped
 
         def second_layer(c):
@@ -222,46 +233,56 @@ def tile_nodelstmcell_pc_t_kernel(tc, h_tilde, k1, k2, k3, t0, t1, W1, b1, W2, b
                 )
             live["k4T", c] = k4T_sb
 
-        def turn_k1(c):
-            k1_sb = live["k1", c]
-            k1T_sb = work.tile([P, ROWS - PLAIN_ROWS, TILES, P], F32, bufs=3)
-            for j in range(PLAIN_ROWS, ROWS):
-                k1T_ps = psum.tile([P, TILES, P], BF16, tag="turned")
+        def turn_slopes(c):
+            halfk1T_ps = psum.tile([P, TILES, P], BF16, tag="turned")
+            for m in range(TILES):
+                nc.tensor.transpose(halfk1T_ps[:, m, :], live["k1", c][:, LAST, m * P : (m + 1) * P], ident_bf16[:])
+            halfk1T_sb = work.tile([P, TILES, P], F32, bufs=3)
+            nc.scalar.activation(out=halfk1T_sb[:], in_=halfk1T_ps[:], func=ACT.Copy, scale=0.5)
+            slopesT_ps = psum.tile([P, 2, TILES, P], BF16, tag="turned")
+            for i, name in enumerate(("k2", "k3")):
                 for m in range(TILES):
-                    nc.tensor.transpose(k1T_ps[:, m, :], k1_sb[:, j, m * P : (m + 1) * P], ident_bf16[:])
-                nc.scalar.copy(out=k1T_sb[:, j - PLAIN_ROWS, :, :], in_=k1T_ps[:])
-            live["k1T", c] = k1T_sb
+                    nc.tensor.transpose(
+                        slopesT_ps[:, i, m, :], live[name, c][:, LAST, m * P : (m + 1) * P], ident_bf16[:]
+                    )
+            slopesT_sb = work.tile([P, 2, TILES, P], F32, bufs=3)
+            nc.scalar.copy(out=slopesT_sb[:], in_=slopesT_ps[:])
+            live["last_slopesT", c] = (halfk1T_sb[:], slopesT_sb[:, 0, :, :], slopesT_sb[:, 1, :, :])
 
         def add_slopes(c):
             total = work.tile([P, ROWS, H], F32, bufs=4)
-            nc.vector.tensor_tensor(out=flat(total), in0=flat(live["k2", c]), in1=flat(live["k3", c]), op=ALU.add)
+            nc.vector.tensor_tensor(
+                out=most(total), in0=most(live["k2", c]), in1=most(live["k3", c]), op=ALU.add
+            )
             live["total", c] = total
 
         def add_state(c):
             total = live["total", c]
             nc.vector.scalar_tensor_tensor(
-                out=flat(total), in0=flat(total), scalar=dt3[:, 0:1], in1=flat(live["ht", c]), op0=ALU.mult, op1=ALU.add
+                out=most(total), in0=most(total), scalar=dt3[:, 0:1], in1=most(live["ht", c]), op0=ALU.mult, op1=ALU.add
             )
 
         def finish(c):
             total = live["total", c]
             for j in range(ROWS):
                 back_ps = psum.tile([P, H], F32, tag="back")
-                if j < PLAIN_ROWS:
-                    nc.tensor.matmul(out=back_ps[:], lhsT=ident_bf16[:], rhs=live["k1", c][:, j, :], start=True, stop=False)
+                if j < LAST:
+                    nc.tensor.matmul(out=back_ps[:], lhsT=half_ident[:], rhs=live["k1", c][:, j, :], start=True, stop=False)
                 else:
-                    for m in range(TILES):
-                        nc.tensor.matmul(
-                            out=back_ps[:, m * P : (m + 1) * P], lhsT=live["k1T", c][:, j - PLAIN_ROWS, m, :],
-                            rhs=ident_f32[:], start=(m == 0), stop=False, is_transpose=True,
-                        )
+                    for i, slopeT in enumerate(live["last_slopesT", c]):
+                        for m in range(TILES):
+                            nc.tensor.matmul(
+                                out=back_ps[:, m * P : (m + 1) * P], lhsT=slopeT[:, m, :], rhs=ident_f32[:],
+                                start=(i == 0 and m == 0), stop=False, is_transpose=True,
+                            )
                 for m in range(TILES):
                     nc.tensor.matmul(
                         out=back_ps[:, m * P : (m + 1) * P], lhsT=live["k4T", c][:, m, j * P : (j + 1) * P],
                         rhs=ident_f32[:], start=False, stop=(m == TILES - 1), is_transpose=True,
                     )
                 nc.vector.scalar_tensor_tensor(
-                    out=total[:, j, :], in0=back_ps[:], scalar=dt6[:, 0:1], in1=total[:, j, :], op0=ALU.mult, op1=ALU.add
+                    out=total[:, j, :], in0=back_ps[:], scalar=dt3[:, 0:1],
+                    in1=live["ht", c][:, j, :] if j == LAST else total[:, j, :], op0=ALU.mult, op1=ALU.add,
                 )
                 nc.sync.dma_start(out=chunk_rows(out, c)[:, j, :], in_=total[:, j, :])
 
@@ -275,16 +296,14 @@ def tile_nodelstmcell_pc_t_kernel(tc, h_tilde, k1, k2, k3, t0, t1, W1, b1, W2, b
         state_to_columns(1)
         quantise_w2()
         for step in range(-1, CHUNKS):
-            for c in chunks_at(step + 1):
-                second_layer(c)
+            for c in chunks_at(step + 3):
+                state_to_columns(c)
             for c in chunks_at(step + 2):
                 first_layer(c)
             for c in chunks_at(step + 1):
                 add_slopes(c)
-            for c in chunks_at(step + 3):
-                state_to_columns(c)
-            for c in chunks_at(step + 1):
-                turn_k1(c)
+                second_layer(c)
+                turn_slopes(c)
             for c in chunks_at(step):
                 add_state(c)
                 finish(c)

@@ -23,7 +23,7 @@ WORDS = H // 2
 STATE_AHEAD = 5
 SLOPE_AHEAD = 3
 LAST = ROWS - 1
-SCALAR_RUNS = 64
+SCALAR_COLS = 256
 
 FLOPS = 2 * 2 * B * H * H
 
@@ -206,10 +206,14 @@ def tile_nodelstmcell_pc_t_kernel(tc, h_tilde, k1, k2, k3, t0, t1, W1, b1, W2, b
                 )
                 nc.scalar.activation(out=zT_sb[:, i, :], in_=pre_ps[:], func=ACT.Tanh, bias=z_bias[:, i : i + 1], scale=1.0)
             z_grouped = work.tile([P, CHUNK * PACK], BF16, align_bytes=64, bufs=3)
-            grouped_view = z_grouped[:].rearrange("p (c r i) -> p c i r", r=4, i=PACK)
-            tile_view = zT_sb[:].rearrange("p i (c r) -> p c i r", r=4)
-            nc.scalar.copy(out=grouped_view[:, 0:SCALAR_RUNS, :, :], in_=tile_view[:, 0:SCALAR_RUNS, :, :])
-            nc.vector.tensor_copy(out=grouped_view[:, SCALAR_RUNS:, :, :], in_=tile_view[:, SCALAR_RUNS:, :, :])
+            nc.scalar.copy(
+                out=z_grouped[:, 0 : SCALAR_COLS * PACK].rearrange("p (c r i) -> p c i r", r=4, i=PACK),
+                in_=zT_sb[:, :, 0:SCALAR_COLS].rearrange("p i (c r) -> p c i r", r=4),
+            )
+            nc.vector.tensor_copy(
+                out=z_grouped[:, SCALAR_COLS * PACK :].rearrange("p (b i) -> p b i", i=PACK),
+                in_=zT_sb[:, :, SCALAR_COLS:].rearrange("p i b -> p b i"),
+            )
             live["z_grouped", c] = z_grouped
 
         def second_layer(c):

@@ -23,7 +23,7 @@ WORDS = H // 2
 STATE_AHEAD = 5
 SLOPE_AHEAD = 3
 LAST = ROWS - 1
-SCALAR_COLS = 256
+SCALAR_COLS = 384
 
 FLOPS = 2 * 2 * B * H * H
 
@@ -75,11 +75,11 @@ def tile_nodelstmcell_pc_t_kernel(tc, h_tilde, k1, k2, k3, t0, t1, W1, b1, W2, b
         w1_sb = const.tile([P, TILES * (H + 2)], BF16)
         w1_rows = w1_sb[:].rearrange("p (i k) -> p i k", k=H + 2)
         nc.sync.dma_start(out=w1_rows[:, :, 0 : H + 1], in_=W1.rearrange("(i p) k -> p i k", p=P))
-        load_state(1)
         bias_rows = const.tile([P, P], BF16)
         nc.vector.memset(bias_rows[:], 0.0)
         nc.sync.dma_start(out=bias_rows[0:TILES, :], in_=b1.rearrange("(i p) -> i p", p=P))
         nc.sync.dma_start(out=bias_rows[TILES : 2 * TILES, :], in_=b2.rearrange("(i p) -> i p", p=P))
+        load_state(1)
         w2_sb = const.tile([P, TILES, H], BF16)
         nc.sync.dma_start(out=w2_sb[:], in_=W2.rearrange("(i p) n -> p i n", p=P))
         load_slopes(0)
@@ -243,15 +243,12 @@ def tile_nodelstmcell_pc_t_kernel(tc, h_tilde, k1, k2, k3, t0, t1, W1, b1, W2, b
                 nc.tensor.transpose(halfk1T_ps[:, m, :], live["k1", c][:, LAST, m * P : (m + 1) * P], ident_bf16[:])
             halfk1T_sb = work.tile([P, TILES, P], F32, bufs=3)
             nc.scalar.activation(out=halfk1T_sb[:], in_=halfk1T_ps[:], func=ACT.Copy, scale=0.5)
-            slopesT_ps = psum.tile([P, 2, TILES, P], BF16, tag="turned")
-            for i, name in enumerate(("k2", "k3")):
-                for m in range(TILES):
-                    nc.tensor.transpose(
-                        slopesT_ps[:, i, m, :], live[name, c][:, LAST, m * P : (m + 1) * P], ident_bf16[:]
-                    )
-            slopesT_sb = work.tile([P, 2, TILES, P], F32, bufs=3)
-            nc.scalar.copy(out=slopesT_sb[:], in_=slopesT_ps[:])
-            live["last_slopesT", c] = (halfk1T_sb[:], slopesT_sb[:, 0, :, :], slopesT_sb[:, 1, :, :])
+            k2T_ps = psum.tile([P, TILES, P], BF16, tag="turned")
+            for m in range(TILES):
+                nc.tensor.transpose(k2T_ps[:, m, :], live["k2", c][:, LAST, m * P : (m + 1) * P], ident_bf16[:])
+            k2T_sb = work.tile([P, TILES, P], F32, bufs=3)
+            nc.scalar.copy(out=k2T_sb[:], in_=k2T_ps[:])
+            live["last_slopesT", c] = (halfk1T_sb[:], k2T_sb[:])
 
         def add_slopes(c):
             total = work.tile([P, ROWS, H], F32, bufs=4)
@@ -263,12 +260,16 @@ def tile_nodelstmcell_pc_t_kernel(tc, h_tilde, k1, k2, k3, t0, t1, W1, b1, W2, b
         def add_state(c):
             total = live["total", c]
             nc.vector.scalar_tensor_tensor(
+                out=total[:, LAST, :], in0=live["k3", c][:, LAST, :], scalar=dt3[:, 0:1], in1=live["ht", c][:, LAST, :],
+                op0=ALU.mult, op1=ALU.add,
+            )
+            nc.vector.scalar_tensor_tensor(
                 out=most(total), in0=most(total), scalar=dt3[:, 0:1], in1=most(live["ht", c]), op0=ALU.mult, op1=ALU.add
             )
 
         def finish(c):
             total = live["total", c]
-            for j in range(ROWS):
+            for j in (0, 1, 3, 2):
                 back_ps = psum.tile([P, H], F32, tag="back")
                 if j < LAST:
                     nc.tensor.matmul(out=back_ps[:], lhsT=half_ident[:], rhs=live["k1", c][:, j, :], start=True, stop=False)
@@ -286,7 +287,7 @@ def tile_nodelstmcell_pc_t_kernel(tc, h_tilde, k1, k2, k3, t0, t1, W1, b1, W2, b
                     )
                 nc.vector.scalar_tensor_tensor(
                     out=total[:, j, :], in0=back_ps[:], scalar=dt3[:, 0:1],
-                    in1=live["ht", c][:, j, :] if j == LAST else total[:, j, :], op0=ALU.mult, op1=ALU.add,
+                    in1=total[:, j, :], op0=ALU.mult, op1=ALU.add,
                 )
                 nc.sync.dma_start(out=chunk_rows(out, c)[:, j, :], in_=total[:, j, :])
 
@@ -299,14 +300,16 @@ def tile_nodelstmcell_pc_t_kernel(tc, h_tilde, k1, k2, k3, t0, t1, W1, b1, W2, b
         first_layer(0)
         state_to_columns(1)
         quantise_w2()
+        state_to_columns(2)
+        add_slopes(0)
         for step in range(-1, CHUNKS):
-            for c in chunks_at(step + 3):
-                state_to_columns(c)
             for c in chunks_at(step + 2):
                 first_layer(c)
+            for c in chunks_at(step + 4):
+                state_to_columns(c)
             for c in chunks_at(step + 1):
-                add_slopes(c)
                 second_layer(c)
+            for c in chunks_at(step + 1):
                 turn_slopes(c)
             for c in chunks_at(step):
                 add_state(c)
@@ -315,3 +318,5 @@ def tile_nodelstmcell_pc_t_kernel(tc, h_tilde, k1, k2, k3, t0, t1, W1, b1, W2, b
                     load_state(later)
                 for later in chunks_at(c + SLOPE_AHEAD):
                     load_slopes(later)
+            for c in chunks_at(step + 2):
+                add_slopes(c)

@@ -22,6 +22,7 @@ CHUNKS = B // CHUNK
 WORDS = H // 2
 STATE_AHEAD = 5
 SLOPE_AHEAD = 3
+TIME_STEP = 16
 LAST = ROWS - 1
 SCALAR_COLS = 384
 
@@ -67,10 +68,10 @@ def tile_nodelstmcell_pc_t_kernel(tc, h_tilde, k1, k2, k3, t0, t1, W1, b1, W2, b
             live["k1", c] = k1_sb
             live["k2", c] = k2_sb
 
-        t0_sb = const.tile([P, 1], BF16)
-        nc.scalar.dma_start(out=t0_sb[:], in_=t0.partition_broadcast(P))
-        t1_sb = const.tile([P, 1], BF16)
-        nc.scalar.dma_start(out=t1_sb[:], in_=t1.partition_broadcast(P))
+        times_sb = const.tile([P, 2 * TIME_STEP], BF16)
+        nc.vector.memset(times_sb[:], 0.0)
+        nc.scalar.dma_start(out=times_sb[0:1, 0:1], in_=t0.rearrange("(p n) -> p n", p=1))
+        nc.scalar.dma_start(out=times_sb[0:1, TIME_STEP : TIME_STEP + 1], in_=t1.rearrange("(p n) -> p n", p=1))
         load_state(0)
         w1_sb = const.tile([P, TILES * (H + 2)], BF16)
         w1_rows = w1_sb[:].rearrange("p (i k) -> p i k", k=H + 2)
@@ -96,10 +97,17 @@ def tile_nodelstmcell_pc_t_kernel(tc, h_tilde, k1, k2, k3, t0, t1, W1, b1, W2, b
         half_ident = const.tile([P, P], BF16)
         nc.vector.tensor_scalar_mul(out=half_ident[:], in0=ident_bf16[:], scalar1=0.5)
 
+        ones = const.tile([P, P], BF16)
+        nc.vector.memset(ones[:], 1.0)
+        times_ps = psum.tile([P, 2 * TIME_STEP], F32, tag="back")
+        nc.tensor.matmul(out=times_ps[:], lhsT=ones[:], rhs=times_sb[:], start=True, stop=True)
+        times = const.tile([P, 2 * TIME_STEP], F32)
+        nc.vector.tensor_copy(out=times[:], in_=times_ps[:])
+        start_time = times[:, 0:1]
         dt = const.tile([P, 1], F32)
-        nc.vector.tensor_tensor(out=dt[:], in0=t1_sb[:], in1=t0_sb[:], op=ALU.subtract)
+        nc.vector.tensor_tensor(out=dt[:], in0=times[:, TIME_STEP : TIME_STEP + 1], in1=start_time, op=ALU.subtract)
         t_end = const.tile([P, 1], F32)
-        nc.vector.tensor_tensor(out=t_end[:], in0=t0_sb[:], in1=dt[:], op=ALU.add)
+        nc.vector.tensor_tensor(out=t_end[:], in0=start_time, in1=dt[:], op=ALU.add)
         dt3 = const.tile([P, 1], F32)
         nc.vector.tensor_scalar_mul(out=dt3[:], in0=dt[:], scalar1=1.0 / 3.0)
 

@@ -23,6 +23,7 @@ WORDS = H // 2
 STATE_AHEAD = 5
 SLOPE_AHEAD = 3
 TIME_STEP = 16
+LAST_TAGS = ("back", "pre", "k4T", "turned")
 LAST = ROWS - 1
 SCALAR_COLS = 384
 
@@ -108,6 +109,8 @@ def tile_nodelstmcell_pc_t_kernel(tc, h_tilde, k1, k2, k3, t0, t1, W1, b1, W2, b
         nc.vector.tensor_tensor(out=dt[:], in0=times[:, TIME_STEP : TIME_STEP + 1], in1=start_time, op=ALU.subtract)
         t_end = const.tile([P, 1], F32)
         nc.vector.tensor_tensor(out=t_end[:], in0=start_time, in1=dt[:], op=ALU.add)
+        dt6 = const.tile([P, 1], F32)
+        nc.vector.tensor_scalar_mul(out=dt6[:], in0=dt[:], scalar1=1.0 / 6.0)
         dt3 = const.tile([P, 1], F32)
         nc.vector.tensor_scalar_mul(out=dt3[:], in0=dt[:], scalar1=1.0 / 3.0)
 
@@ -246,17 +249,15 @@ def tile_nodelstmcell_pc_t_kernel(tc, h_tilde, k1, k2, k3, t0, t1, W1, b1, W2, b
             live["k4T", c] = k4T_sb
 
         def turn_slopes(c):
-            halfk1T_ps = psum.tile([P, TILES, P], BF16, tag="turned")
-            for m in range(TILES):
-                nc.tensor.transpose(halfk1T_ps[:, m, :], live["k1", c][:, LAST, m * P : (m + 1) * P], ident_bf16[:])
-            halfk1T_sb = work.tile([P, TILES, P], F32, bufs=3)
-            nc.scalar.activation(out=halfk1T_sb[:], in_=halfk1T_ps[:], func=ACT.Copy, scale=0.5)
-            k2T_ps = psum.tile([P, TILES, P], BF16, tag="turned")
-            for m in range(TILES):
-                nc.tensor.transpose(k2T_ps[:, m, :], live["k2", c][:, LAST, m * P : (m + 1) * P], ident_bf16[:])
-            k2T_sb = work.tile([P, TILES, P], F32, bufs=3)
-            nc.scalar.copy(out=k2T_sb[:], in_=k2T_ps[:])
-            live["last_slopesT", c] = (halfk1T_sb[:], k2T_sb[:])
+            slopesT_ps = psum.tile([P, 2, TILES, P], BF16, tag="turned")
+            for i, name in enumerate(("k2", "k3")):
+                for m in range(TILES):
+                    nc.tensor.transpose(
+                        slopesT_ps[:, i, m, :], live[name, c][:, LAST, m * P : (m + 1) * P], ident_bf16[:]
+                    )
+            slopesT_sb = work.tile([P, 2, TILES, P], F32, bufs=3)
+            nc.scalar.copy(out=slopesT_sb[:], in_=slopesT_ps[:])
+            live["last_slopesT", c] = (slopesT_sb[:, 0, :, :], slopesT_sb[:, 1, :, :])
 
         def add_slopes(c):
             total = work.tile([P, ROWS, H], F32, bufs=4)
@@ -268,7 +269,7 @@ def tile_nodelstmcell_pc_t_kernel(tc, h_tilde, k1, k2, k3, t0, t1, W1, b1, W2, b
         def add_state(c):
             total = live["total", c]
             nc.vector.scalar_tensor_tensor(
-                out=total[:, LAST, :], in0=live["k3", c][:, LAST, :], scalar=dt3[:, 0:1], in1=live["ht", c][:, LAST, :],
+                out=total[:, LAST, :], in0=live["k1", c][:, LAST, :], scalar=dt6[:, 0:1], in1=live["ht", c][:, LAST, :],
                 op0=ALU.mult, op1=ALU.add,
             )
             nc.vector.scalar_tensor_tensor(
@@ -277,8 +278,9 @@ def tile_nodelstmcell_pc_t_kernel(tc, h_tilde, k1, k2, k3, t0, t1, W1, b1, W2, b
 
         def finish(c):
             total = live["total", c]
-            for j in (0, 1, 3, 2):
-                back_ps = psum.tile([P, H], F32, tag="back")
+            for j in range(ROWS):
+                tag = LAST_TAGS[j] if c == CHUNKS - 1 else "back"
+                back_ps = psum.tile([P, H], F32, tag=tag)
                 if j < LAST:
                     nc.tensor.matmul(out=back_ps[:], lhsT=half_ident[:], rhs=live["k1", c][:, j, :], start=True, stop=False)
                 else:
@@ -313,12 +315,6 @@ def tile_nodelstmcell_pc_t_kernel(tc, h_tilde, k1, k2, k3, t0, t1, W1, b1, W2, b
         for step in range(-1, CHUNKS):
             for c in chunks_at(step + 2):
                 first_layer(c)
-            for c in chunks_at(step + 4):
-                state_to_columns(c)
-            for c in chunks_at(step + 1):
-                second_layer(c)
-            for c in chunks_at(step + 1):
-                turn_slopes(c)
             for c in chunks_at(step):
                 add_state(c)
                 finish(c)
@@ -326,5 +322,11 @@ def tile_nodelstmcell_pc_t_kernel(tc, h_tilde, k1, k2, k3, t0, t1, W1, b1, W2, b
                     load_state(later)
                 for later in chunks_at(c + SLOPE_AHEAD):
                     load_slopes(later)
+            for c in chunks_at(step + 1):
+                second_layer(c)
             for c in chunks_at(step + 2):
                 add_slopes(c)
+            for c in chunks_at(step + 1):
+                turn_slopes(c)
+            for c in chunks_at(step + 4):
+                state_to_columns(c)

@@ -50,30 +50,35 @@ def tile_nodelstmcell_pc_t_kernel(tc, h_tilde, k1, k2, k3, t0, t1, W1, b1, W2, b
         def most(tile3):
             return flat(tile3[:, 0:LAST, :])
 
+        drams = {"h_tilde": h_tilde, "k1": k1, "k2": k2, "k3": k3}
+        live_names = {"h_tilde": "ht", "k1": "k1", "k2": "k2", "k3": "k3"}
+
+        def load(name, c, first=0, last=ROWS):
+            if first == 0:
+                pool = states if name in ("h_tilde", "k3") else slopes
+                tile = pool.tile([P, ROWS, H], BF16, name=name + "_sb")
+                live[live_names[name], c] = tile
+            nc.sync.dma_start(
+                out=live[live_names[name], c][:, first:last, :], in_=chunk_rows(drams[name], c)[:, first:last, :]
+            )
+
         def load_state(c):
-            k3_sb = states.tile([P, ROWS, H], BF16)
-            ht_sb = states.tile([P, ROWS, H], BF16)
-            parts = 2 if c == 0 else 1
-            for part in range(parts):
-                rows = slice(part * ROWS // parts, (part + 1) * ROWS // parts)
-                nc.sync.dma_start(out=k3_sb[:, rows, :], in_=chunk_rows(k3, c)[:, rows, :])
-                nc.sync.dma_start(out=ht_sb[:, rows, :], in_=chunk_rows(h_tilde, c)[:, rows, :])
-            live["k3", c] = k3_sb
-            live["ht", c] = ht_sb
+            load("k3", c)
+            load("h_tilde", c)
 
         def load_slopes(c):
-            k1_sb = slopes.tile([P, ROWS, H], BF16)
-            nc.sync.dma_start(out=k1_sb[:], in_=chunk_rows(k1, c))
-            k2_sb = slopes.tile([P, ROWS, H], BF16)
-            nc.sync.dma_start(out=k2_sb[:], in_=chunk_rows(k2, c))
-            live["k1", c] = k1_sb
-            live["k2", c] = k2_sb
+            load("k1", c)
+            load("k2", c)
 
         times_sb = const.tile([P, 2 * TIME_STEP], BF16)
         nc.vector.memset(times_sb[:], 0.0)
         nc.scalar.dma_start(out=times_sb[0:1, 0:1], in_=t0.rearrange("(p n) -> p n", p=1))
         nc.scalar.dma_start(out=times_sb[0:1, TIME_STEP : TIME_STEP + 1], in_=t1.rearrange("(p n) -> p n", p=1))
-        load_state(0)
+        for first in (0, ROWS // 2):
+            load("k3", 0, first, first + ROWS // 2)
+            load("k2", 0, first, first + ROWS // 2)
+        for first in (0, ROWS // 2):
+            load("h_tilde", 0, first, first + ROWS // 2)
         w1_sb = const.tile([P, TILES * (H + 2)], BF16)
         w1_rows = w1_sb[:].rearrange("p (i k) -> p i k", k=H + 2)
         nc.sync.dma_start(out=w1_rows[:, :, 0 : H + 1], in_=W1.rearrange("(i p) k -> p i k", p=P))
@@ -84,7 +89,7 @@ def tile_nodelstmcell_pc_t_kernel(tc, h_tilde, k1, k2, k3, t0, t1, W1, b1, W2, b
         load_state(1)
         w2_sb = const.tile([P, TILES, H], BF16)
         nc.sync.dma_start(out=w2_sb[:], in_=W2.rearrange("(i p) n -> p i n", p=P))
-        load_slopes(0)
+        load("k1", 0)
         load_state(2)
         load_slopes(1)
         load_state(3)
@@ -248,30 +253,45 @@ def tile_nodelstmcell_pc_t_kernel(tc, h_tilde, k1, k2, k3, t0, t1, W1, b1, W2, b
                 )
             live["k4T", c] = k4T_sb
 
+        def adds_k1(c, j):
+            return j < LAST or c == CHUNKS - 1
+
+        def turned_slopes(c):
+            return ("k2", "k3")
+
         def turn_slopes(c):
+            names = turned_slopes(c)
             slopesT_ps = psum.tile([P, 2, TILES, P], BF16, tag="turned")
-            for i, name in enumerate(("k2", "k3")):
+            for i, name in enumerate(names):
                 for m in range(TILES):
                     nc.tensor.transpose(
                         slopesT_ps[:, i, m, :], live[name, c][:, LAST, m * P : (m + 1) * P], ident_bf16[:]
                     )
             slopesT_sb = work.tile([P, 2, TILES, P], F32, bufs=3)
-            nc.scalar.copy(out=slopesT_sb[:], in_=slopesT_ps[:])
-            live["last_slopesT", c] = (slopesT_sb[:, 0, :, :], slopesT_sb[:, 1, :, :])
+            nc.scalar.copy(out=slopesT_sb[:, 0 : len(names), :, :], in_=slopesT_ps[:, 0 : len(names), :, :])
+            live["last_slopesT", c] = [slopesT_sb[:, i, :, :] for i in range(len(names))]
 
         def add_slopes(c):
             total = work.tile([P, ROWS, H], F32, bufs=4)
-            nc.vector.tensor_tensor(
-                out=most(total), in0=most(live["k2", c]), in1=most(live["k3", c]), op=ALU.add
-            )
+            cuts = (0, ROWS // 2, LAST) if c == 0 else (0, LAST)
+            for first, last in zip(cuts, cuts[1:]):
+                nc.vector.tensor_tensor(
+                    out=flat(total[:, first:last, :]), in0=flat(live["k2", c][:, first:last, :]),
+                    in1=flat(live["k3", c][:, first:last, :]), op=ALU.add,
+                )
             live["total", c] = total
 
         def add_state(c):
             total = live["total", c]
-            nc.vector.scalar_tensor_tensor(
-                out=total[:, LAST, :], in0=live["k1", c][:, LAST, :], scalar=dt6[:, 0:1], in1=live["ht", c][:, LAST, :],
-                op0=ALU.mult, op1=ALU.add,
-            )
+            rest = live["ht", c][:, LAST, :]
+            for name, factor in (("k1", dt6), ("k3", dt3)):
+                if not (name in turned_slopes(c) or name == "k1" and adds_k1(c, LAST)):
+                    nc.vector.scalar_tensor_tensor(
+                        out=total[:, LAST, :], in0=live[name, c][:, LAST, :], scalar=factor[:, 0:1], in1=rest,
+                        op0=ALU.mult, op1=ALU.add,
+                    )
+                    rest = total[:, LAST, :]
+            live["last_rest", c] = rest
             nc.vector.scalar_tensor_tensor(
                 out=most(total), in0=most(total), scalar=dt3[:, 0:1], in1=most(live["ht", c]), op0=ALU.mult, op1=ALU.add
             )
@@ -281,14 +301,14 @@ def tile_nodelstmcell_pc_t_kernel(tc, h_tilde, k1, k2, k3, t0, t1, W1, b1, W2, b
             for j in range(ROWS):
                 tag = LAST_TAGS[j] if c == CHUNKS - 1 else "back"
                 back_ps = psum.tile([P, H], F32, tag=tag)
-                if j < LAST:
+                if adds_k1(c, j):
                     nc.tensor.matmul(out=back_ps[:], lhsT=half_ident[:], rhs=live["k1", c][:, j, :], start=True, stop=False)
-                else:
+                if j == LAST:
                     for i, slopeT in enumerate(live["last_slopesT", c]):
                         for m in range(TILES):
                             nc.tensor.matmul(
                                 out=back_ps[:, m * P : (m + 1) * P], lhsT=slopeT[:, m, :], rhs=ident_f32[:],
-                                start=(i == 0 and m == 0), stop=False, is_transpose=True,
+                                start=(i == 0 and m == 0 and not adds_k1(c, j)), stop=False, is_transpose=True,
                             )
                 for m in range(TILES):
                     nc.tensor.matmul(
@@ -297,13 +317,15 @@ def tile_nodelstmcell_pc_t_kernel(tc, h_tilde, k1, k2, k3, t0, t1, W1, b1, W2, b
                     )
                 nc.vector.scalar_tensor_tensor(
                     out=total[:, j, :], in0=back_ps[:], scalar=dt3[:, 0:1],
-                    in1=total[:, j, :], op0=ALU.mult, op1=ALU.add,
+                    in1=live["last_rest", c] if j == LAST else total[:, j, :], op0=ALU.mult, op1=ALU.add,
                 )
                 nc.sync.dma_start(out=chunk_rows(out, c)[:, j, :], in_=total[:, j, :])
 
         def chunks_at(c):
             return [c] if 0 <= c < CHUNKS else []
 
+        add_slopes(0)
+        turn_slopes(0)
         state_to_columns(0)
         quantise_w1()
         biases_to_partitions()
@@ -311,7 +333,6 @@ def tile_nodelstmcell_pc_t_kernel(tc, h_tilde, k1, k2, k3, t0, t1, W1, b1, W2, b
         state_to_columns(1)
         quantise_w2()
         state_to_columns(2)
-        add_slopes(0)
         for step in range(-1, CHUNKS):
             for c in chunks_at(step + 2):
                 first_layer(c)
@@ -327,6 +348,7 @@ def tile_nodelstmcell_pc_t_kernel(tc, h_tilde, k1, k2, k3, t0, t1, W1, b1, W2, b
             for c in chunks_at(step + 2):
                 add_slopes(c)
             for c in chunks_at(step + 1):
-                turn_slopes(c)
+                if c > 0:
+                    turn_slopes(c)
             for c in chunks_at(step + 4):
                 state_to_columns(c)

@@ -22,7 +22,6 @@ CHUNKS = B // CHUNK
 WORDS = H // 2
 STATE_AHEAD = 5
 SLOPE_AHEAD = 3
-TIME_STEP = 16
 LAST_TAGS = ("back", "pre", "k4T", "turned")
 LAST = ROWS - 1
 SCALAR_COLS = 384
@@ -70,15 +69,15 @@ def tile_nodelstmcell_pc_t_kernel(tc, h_tilde, k1, k2, k3, t0, t1, W1, b1, W2, b
             load("k1", c)
             load("k2", c)
 
-        times_sb = const.tile([P, 2 * TIME_STEP], BF16)
-        nc.vector.memset(times_sb[:], 0.0)
-        nc.scalar.dma_start(out=times_sb[0:1, 0:1], in_=t0.rearrange("(p n) -> p n", p=1))
-        nc.scalar.dma_start(out=times_sb[0:1, TIME_STEP : TIME_STEP + 1], in_=t1.rearrange("(p n) -> p n", p=1))
+        t0_sb = const.tile([P, 1], BF16)
+        nc.scalar.dma_start(out=t0_sb[:], in_=t0.partition_broadcast(P))
+        t1_sb = const.tile([P, 1], BF16)
+        nc.scalar.dma_start(out=t1_sb[:], in_=t1.partition_broadcast(P))
         for first in (0, ROWS // 2):
             load("k3", 0, first, first + ROWS // 2)
-            load("k2", 0, first, first + ROWS // 2)
-        for first in (0, ROWS // 2):
             load("h_tilde", 0, first, first + ROWS // 2)
+        for first in (0, ROWS // 2):
+            load("k2", 0, first, first + ROWS // 2)
         w1_sb = const.tile([P, TILES * (H + 2)], BF16)
         w1_rows = w1_sb[:].rearrange("p (i k) -> p i k", k=H + 2)
         nc.sync.dma_start(out=w1_rows[:, :, 0 : H + 1], in_=W1.rearrange("(i p) k -> p i k", p=P))
@@ -103,17 +102,10 @@ def tile_nodelstmcell_pc_t_kernel(tc, h_tilde, k1, k2, k3, t0, t1, W1, b1, W2, b
         half_ident = const.tile([P, P], BF16)
         nc.vector.tensor_scalar_mul(out=half_ident[:], in0=ident_bf16[:], scalar1=0.5)
 
-        ones = const.tile([P, P], BF16)
-        nc.vector.memset(ones[:], 1.0)
-        times_ps = psum.tile([P, 2 * TIME_STEP], F32, tag="back")
-        nc.tensor.matmul(out=times_ps[:], lhsT=ones[:], rhs=times_sb[:], start=True, stop=True)
-        times = const.tile([P, 2 * TIME_STEP], F32)
-        nc.vector.tensor_copy(out=times[:], in_=times_ps[:])
-        start_time = times[:, 0:1]
         dt = const.tile([P, 1], F32)
-        nc.vector.tensor_tensor(out=dt[:], in0=times[:, TIME_STEP : TIME_STEP + 1], in1=start_time, op=ALU.subtract)
+        nc.vector.tensor_tensor(out=dt[:], in0=t1_sb[:], in1=t0_sb[:], op=ALU.subtract)
         t_end = const.tile([P, 1], F32)
-        nc.vector.tensor_tensor(out=t_end[:], in0=start_time, in1=dt[:], op=ALU.add)
+        nc.vector.tensor_tensor(out=t_end[:], in0=t0_sb[:], in1=dt[:], op=ALU.add)
         dt6 = const.tile([P, 1], F32)
         nc.vector.tensor_scalar_mul(out=dt6[:], in0=dt[:], scalar1=1.0 / 6.0)
         dt3 = const.tile([P, 1], F32)

from contextlib import ExitStack

import concourse.mybir as mybir
from concourse.masks import make_identity

F32 = mybir.dt.float32
BF16 = mybir.dt.bfloat16
U32 = mybir.dt.uint32
U8 = mybir.dt.uint8
FP8X4 = mybir.dt.float8_e4m3fn_x4
ALU = mybir.AluOpType
ACT = mybir.ActivationFunctionType

P = 128
B = 4096
H = 512
PACK = 4
TILES = H // P
ROWS = 4
CHUNK = P * ROWS
CHUNKS = B // CHUNK
WORDS = H // 2
STATE_AHEAD = 5
SLOPE_AHEAD = 3
LAST_TAGS = ("back", "pre", "k4T", "turned")
LAST = ROWS - 1
SCALAR_COLS = 384

FLOPS = 2 * 2 * B * H * H


def tile_nodelstmcell_pc_t_kernel(tc, h_tilde, k1, k2, k3, t0, t1, W1, b1, W2, b2, out):
    nc = tc.nc
    with ExitStack() as stack:
        const = stack.enter_context(tc.tile_pool(name="const", bufs=1))
        states = stack.enter_context(tc.tile_pool(name="states", bufs=STATE_AHEAD))
        slopes = stack.enter_context(tc.tile_pool(name="slopes", bufs=SLOPE_AHEAD))
        work = stack.enter_context(tc.tile_pool(name="work", bufs=2))
        psum = stack.enter_context(tc.psum_pool(name="psum", bufs=2))

        live = {}

        def chunk_rows(dram, c):
            return dram[c * CHUNK : (c + 1) * CHUNK, :].rearrange("(p j) n -> p j n", j=ROWS)

        def flat(rows):
            return rows.rearrange("p j n -> p (j n)")

        def most(tile3):
            return flat(tile3[:, 0:LAST, :])

        drams = {"h_tilde": h_tilde, "k1": k1, "k2": k2, "k3": k3}
        live_names = {"h_tilde": "ht", "k1": "k1", "k2": "k2", "k3": "k3"}

        def load(name, c, first=0, last=ROWS):
            if first == 0:
                pool = states if name in ("h_tilde", "k3") else slopes
                tile = pool.tile([P, ROWS, H], BF16, name=name + "_sb")
                live[live_names[name], c] = tile
            nc.sync.dma_start(
                out=live[live_names[name], c][:, first:last, :], in_=chunk_rows(drams[name], c)[:, first:last, :]
            )

        def load_state(c):
            load("k3", c)
            load("h_tilde", c)

        def load_slopes(c):
            load("k1", c)
            load("k2", c)

        t0_sb = const.tile([P, 1], BF16)
        nc.scalar.dma_start(out=t0_sb[:], in_=t0.partition_broadcast(P))
        t1_sb = const.tile([P, 1], BF16)
        nc.scalar.dma_start(out=t1_sb[:], in_=t1.partition_broadcast(P))
        for first in (0, ROWS // 2):
            load("k3", 0, first, first + ROWS // 2)
            load("h_tilde", 0, first, first + ROWS // 2)
        for first in (0, ROWS // 2):
            load("k2", 0, first, first + ROWS // 2)
        w1_sb = const.tile([P, TILES * (H + 2)], BF16)
        w1_rows = w1_sb[:].rearrange("p (i k) -> p i k", k=H + 2)
        nc.sync.dma_start(out=w1_rows[:, :, 0 : H + 1], in_=W1.rearrange("(i p) k -> p i k", p=P))
        bias_rows = const.tile([P, P], BF16)
        nc.vector.memset(bias_rows[:], 0.0)
        nc.sync.dma_start(out=bias_rows[0:TILES, :], in_=b1.rearrange("(i p) -> i p", p=P))
        nc.sync.dma_start(out=bias_rows[TILES : 2 * TILES, :], in_=b2.rearrange("(i p) -> i p", p=P))
        load_state(1)
        w2_sb = const.tile([P, TILES, H], BF16)
        nc.sync.dma_start(out=w2_sb[:], in_=W2.rearrange("(i p) n -> p i n", p=P))
        load("k1", 0)
        load_state(2)
        load_slopes(1)
        load_state(3)
        load_slopes(2)
        load_state(4)

        ident_f32 = const.tile([P, P], F32)
        make_identity(nc, ident_f32[:])
        ident_bf16 = const.tile([P, P], BF16)
        make_identity(nc, ident_bf16[:])
        half_ident = const.tile([P, P], BF16)
        nc.vector.tensor_scalar_mul(out=half_ident[:], in0=ident_bf16[:], scalar1=0.5)

        dt = const.tile([P, 1], F32)
        nc.vector.tensor_tensor(out=dt[:], in0=t1_sb[:], in1=t0_sb[:], op=ALU.subtract)
        t_end = const.tile([P, 1], F32)
        nc.vector.tensor_tensor(out=t_end[:], in0=t0_sb[:], in1=dt[:], op=ALU.add)
        dt6 = const.tile([P, 1], F32)
        nc.vector.tensor_scalar_mul(out=dt6[:], in0=dt[:], scalar1=1.0 / 6.0)
        dt3 = const.tile([P, 1], F32)
        nc.vector.tensor_scalar_mul(out=dt3[:], in0=dt[:], scalar1=1.0 / 3.0)

        w1_codes = const.tile([P, H], U32, align_bytes=64)
        w1_scales = const.tile([P, H], U8, align_bytes=64)
        w2_codes = const.tile([P, H], U32, align_bytes=64)
        w2_scales = const.tile([P, H], U8, align_bytes=64)
        z_bias = const.tile([P, TILES], F32)
        k4_bias = const.tile([P, TILES], F32)

        def quantise_w1():
            w1_words = w1_sb[:].bitcast(F32)
            w1_grouped = const.tile([P, H * PACK], BF16, align_bytes=64)
            w1_grouped_words = w1_grouped[:].bitcast(F32).rearrange("q (n u) -> q n u", u=2)
            for half in range(2):
                w1T_ps = psum.tile([P, 2, 2 * P], F32, tag="turned")
                for i in range(2):
                    first = (2 * half + i) * (WORDS + 1)
                    for u in range(2):
                        nc.tensor.transpose(
                            w1T_ps[:, u, i * P : (i + 1) * P],
                            w1_words[:, first + u * P : first + (u + 1) * P],
                            ident_f32[:],
                        )
                nc.scalar.copy(
                    out=w1_grouped_words[:, half * 2 * P : (half + 1) * 2 * P, :],
                    in_=w1T_ps[:].rearrange("q u n -> q n u"),
                )
            nc.vector.quantize_mx(out=w1_codes[:].bitcast(FP8X4), scales=w1_scales[:], in_=w1_grouped[:])

        def quantise_w2():
            w2_grouped = const.tile([P, H * PACK], BF16, align_bytes=64)
            w2_grouped_cols = w2_grouped[:].rearrange("p (o i) -> p o i", i=PACK)
            for half in range(2):
                w2T_ps = psum.tile([P, PACK, 2 * P], BF16, tag="turned")
                for m in range(2):
                    for i in range(PACK):
                        nc.tensor.transpose(
                            w2T_ps[:, i, m * P : (m + 1) * P],
                            w2_sb[:, 2 * half + m, i * P : (i + 1) * P],
                            ident_bf16[:],
                        )
                nc.scalar.activation(
                    out=w2_grouped_cols[:, half * 2 * P : (half + 1) * 2 * P, :],
                    in_=w2T_ps[:].rearrange("p i o -> p o i"),
                    func=ACT.Copy,
                    scale=0.5,
                )
            nc.vector.quantize_mx(out=w2_codes[:].bitcast(FP8X4), scales=w2_scales[:], in_=w2_grouped[:])

        def biases_to_partitions():
            biasT_ps = psum.tile([P, P], BF16, tag="turned")
            nc.tensor.transpose(biasT_ps[:], bias_rows[:], ident_bf16[:])
            bias_cols = const.tile([P, 2 * TILES], F32)
            nc.vector.tensor_copy(out=bias_cols[:], in_=biasT_ps[:, 0 : 2 * TILES])
            nc.vector.scalar_tensor_tensor(
                out=z_bias[:], in0=w1_rows[:, :, H], scalar=t_end[:, 0:1], in1=bias_cols[:, 0:TILES],
                op0=ALU.mult, op1=ALU.add,
            )
            nc.vector.tensor_scalar_mul(out=k4_bias[:], in0=bias_cols[:, TILES : 2 * TILES], scalar1=0.5)

        def state_to_columns(c):
            y_sb = work.tile([P, ROWS * H], BF16)
            for half in range(2):
                rows = slice(2 * half, 2 * half + 2)
                nc.vector.scalar_tensor_tensor(
                    out=y_sb[:, 2 * half * H : 2 * (half + 1) * H], in0=flat(live["k3", c][:, rows, :]), scalar=dt[:, 0:1],
                    in1=flat(live["ht", c][:, rows, :]), op0=ALU.mult, op1=ALU.add,
                )
            y_words = y_sb[:].bitcast(F32)
            y_grouped = work.tile([P, CHUNK * PACK], BF16, align_bytes=64, bufs=3)
            y_grouped_words = y_grouped[:].bitcast(F32).rearrange("q (b u) -> q b u", u=2)
            for half in range(2):
                yT_ps = psum.tile([P, 2, 2 * P], F32, tag="turned")
                for i in range(2):
                    first = (2 * half + i) * WORDS
                    for u in range(2):
                        nc.tensor.transpose(
                            yT_ps[:, u, i * P : (i + 1) * P],
                            y_words[:, first + u * P : first + (u + 1) * P],
                            ident_f32[:],
                        )
                nc.scalar.copy(
                    out=y_grouped_words[:, half * 2 * P : (half + 1) * 2 * P, :],
                    in_=yT_ps[:].rearrange("q u b -> q b u"),
                )
            live["y_grouped", c] = y_grouped

        def first_layer(c):
            y_codes = work.tile([P, CHUNK], U32, align_bytes=64)
            y_scales = work.tile([P, CHUNK], U8, align_bytes=64)
            nc.vector.quantize_mx(out=y_codes[:].bitcast(FP8X4), scales=y_scales[:], in_=live["y_grouped", c][:])
            zT_sb = work.tile([P, PACK, CHUNK], BF16)
            for i in range(TILES):
                pre_ps = psum.tile([P, CHUNK], F32, tag="pre")
                nc.tensor.matmul_mx(
                    out=pre_ps[:],
                    lhsT=w1_codes[:, i * P : (i + 1) * P].bitcast(FP8X4),
                    lhsT_scale=w1_scales[:, i * P : (i + 1) * P],
                    rhs=y_codes[:].bitcast(FP8X4),
                    rhs_scale=y_scales[:],
                    start=True,
                    stop=True,
                )
                nc.scalar.activation(out=zT_sb[:, i, :], in_=pre_ps[:], func=ACT.Tanh, bias=z_bias[:, i : i + 1], scale=1.0)
            z_grouped = work.tile([P, CHUNK * PACK], BF16, align_bytes=64, bufs=3)
            nc.scalar.copy(
                out=z_grouped[:, 0 : SCALAR_COLS * PACK].rearrange("p (c r i) -> p c i r", r=4, i=PACK),
                in_=zT_sb[:, :, 0:SCALAR_COLS].rearrange("p i (c r) -> p c i r", r=4),
            )
            nc.vector.tensor_copy(
                out=z_grouped[:, SCALAR_COLS * PACK :].rearrange("p (b i) -> p b i", i=PACK),
                in_=zT_sb[:, :, SCALAR_COLS:].rearrange("p i b -> p b i"),
            )
            live["z_grouped", c] = z_grouped

        def second_layer(c):
            z_codes = work.tile([P, CHUNK], U32, align_bytes=64)
            z_scales = work.tile([P, CHUNK], U8, align_bytes=64)
            nc.vector.quantize_mx(out=z_codes[:].bitcast(FP8X4), scales=z_scales[:], in_=live["z_grouped", c][:])
            k4T_sb = work.tile([P, TILES, CHUNK], F32, bufs=3)
            for m in range(TILES):
                k4T_ps = psum.tile([P, CHUNK], F32, tag="k4T")
                nc.tensor.matmul_mx(
                    out=k4T_ps[:],
                    lhsT=w2_codes[:, m * P : (m + 1) * P].bitcast(FP8X4),
                    lhsT_scale=w2_scales[:, m * P : (m + 1) * P],
                    rhs=z_codes[:].bitcast(FP8X4),
                    rhs_scale=z_scales[:],
                    start=True,
                    stop=True,
                )
                nc.scalar.activation(
                    out=k4T_sb[:, m, :], in_=k4T_ps[:], func=ACT.Identity, bias=k4_bias[:, m : m + 1], scale=1.0
                )
            live["k4T", c] = k4T_sb

        def adds_k1(c, j):
            return j < LAST or c == CHUNKS - 1

        def turned_slopes(c):
            return ("k2", "k3")

        def turn_slopes(c):
            names = turned_slopes(c)
            slopesT_ps = psum.tile([P, 2, TILES, P], BF16, tag="turned")
            for i, name in enumerate(names):
                for m in range(TILES):
                    nc.tensor.transpose(
                        slopesT_ps[:, i, m, :], live[name, c][:, LAST, m * P : (m + 1) * P], ident_bf16[:]
                    )
            slopesT_sb = work.tile([P, 2, TILES, P], F32, bufs=3)
            nc.scalar.copy(out=slopesT_sb[:, 0 : len(names), :, :], in_=slopesT_ps[:, 0 : len(names), :, :])
            live["last_slopesT", c] = [slopesT_sb[:, i, :, :] for i in range(len(names))]

        def add_slopes(c):
            total = work.tile([P, ROWS, H], F32, bufs=4)
            cuts = (0, ROWS // 2, LAST) if c == 0 else (0, LAST)
            for first, last in zip(cuts, cuts[1:]):
                nc.vector.tensor_tensor(
                    out=flat(total[:, first:last, :]), in0=flat(live["k2", c][:, first:last, :]),
                    in1=flat(live["k3", c][:, first:last, :]), op=ALU.add,
                )
            live["total", c] = total

        def add_state(c):
            total = live["total", c]
            rest = live["ht", c][:, LAST, :]
            for name, factor in (("k1", dt6), ("k3", dt3)):
                if not (name in turned_slopes(c) or name == "k1" and adds_k1(c, LAST)):
                    nc.vector.scalar_tensor_tensor(
                        out=total[:, LAST, :], in0=live[name, c][:, LAST, :], scalar=factor[:, 0:1], in1=rest,
                        op0=ALU.mult, op1=ALU.add,
                    )
                    rest = total[:, LAST, :]
            live["last_rest", c] = rest
            nc.vector.scalar_tensor_tensor(
                out=most(total), in0=most(total), scalar=dt3[:, 0:1], in1=most(live["ht", c]), op0=ALU.mult, op1=ALU.add
            )

        def finish(c):
            total = live["total", c]
            for j in range(ROWS):
                tag = LAST_TAGS[j] if c == CHUNKS - 1 else "back"
                back_ps = psum.tile([P, H], F32, tag=tag)
                if adds_k1(c, j):
                    nc.tensor.matmul(out=back_ps[:], lhsT=half_ident[:], rhs=live["k1", c][:, j, :], start=True, stop=False)
                if j == LAST:
                    for i, slopeT in enumerate(live["last_slopesT", c]):
                        for m in range(TILES):
                            nc.tensor.matmul(
                                out=back_ps[:, m * P : (m + 1) * P], lhsT=slopeT[:, m, :], rhs=ident_f32[:],
                                start=(i == 0 and m == 0 and not adds_k1(c, j)), stop=False, is_transpose=True,
                            )
                for m in range(TILES):
                    nc.tensor.matmul(
                        out=back_ps[:, m * P : (m + 1) * P], lhsT=live["k4T", c][:, m, j * P : (j + 1) * P],
                        rhs=ident_f32[:], start=False, stop=(m == TILES - 1), is_transpose=True,
                    )
                nc.vector.scalar_tensor_tensor(
                    out=total[:, j, :], in0=back_ps[:], scalar=dt3[:, 0:1],
                    in1=live["last_rest", c] if j == LAST else total[:, j, :], op0=ALU.mult, op1=ALU.add,
                )
                nc.sync.dma_start(out=chunk_rows(out, c)[:, j, :], in_=total[:, j, :])

        def chunks_at(c):
            return [c] if 0 <= c < CHUNKS else []

        add_slopes(0)
        turn_slopes(0)
        state_to_columns(0)
        quantise_w1()
        biases_to_partitions()
        first_layer(0)
        state_to_columns(1)
        quantise_w2()
        state_to_columns(2)
        for step in range(-1, CHUNKS):
            for c in chunks_at(step + 2):
                first_layer(c)
            for c in chunks_at(step):
                add_state(c)
                finish(c)
                for later in chunks_at(c + STATE_AHEAD):
                    load_state(later)
                for later in chunks_at(c + SLOPE_AHEAD):
                    load_slopes(later)
            for c in chunks_at(step + 1):
                second_layer(c)
            for c in chunks_at(step + 2):
                add_slopes(c)
            for c in chunks_at(step + 1):
                if c > 0:
                    turn_slopes(c)
            for c in chunks_at(step + 4):
                state_to_columns(c)
